import numpy as np
import ml_dtypes

BF16 = ml_dtypes.bfloat16


def bf(x):
    return np.asarray(x, np.float32).astype(BF16)


def f32(x):
    return np.asarray(x, np.float32)


def f64(x):
    return np.asarray(x).astype(np.float64)


def striped(idx):
    return np.tile(idx.reshape(-1, 16).T, (8, 1))


D, S, M, H, R, N = 128, 256, 128, 128, 16, 2048
EPS = 1e-5
SLOPE = 0.2


def setup_inputs():
    return {"table": bf(np.random.standard_normal((D, S))), "w": bf(np.random.standard_normal((D, M)) / np.sqrt(D)), "b": f32(0.1 * np.random.standard_normal((M, 1))), "ls": f32(1.0 + 0.1 * np.random.standard_normal((M, 1))), "lb": f32(0.1 * np.random.standard_normal((M, 1))), "offs": striped(np.concatenate([np.random.permutation(S)[:H] for _ in range(R)]))}


def reference(table, w, b, ls, lb, offs):
    idx = offs[:16].T.reshape(-1)
    z = f64(w).T @ f64(table)[:, idx] + f64(b)
    mu = z.mean(axis=0, keepdims=True)
    var = ((z - mu) ** 2).mean(axis=0, keepdims=True)
    y = (z - mu) / np.sqrt(var + EPS) * f64(ls) + f64(lb)
    return np.maximum(y, SLOPE * y)

@@ -1,0 +1,81 @@
+import concourse.mybir as mybir
+
+F32, BF16, U16 = mybir.dt.float32, mybir.dt.bfloat16, mybir.dt.uint16
+ACT = mybir.ActivationFunctionType
+ALU = mybir.AluOpType
+AX = mybir.AxisListType
+
+P = 128
+POINTS = 256
+N = 2048
+PIECE = 256
+CHUNK = 512
+CHUNKS = N // CHUNK
+EPS = 1e-5
+SLOPE = 0.2
+
+FLOPS = 2 * P * P * N
+
+
+def tile_lfa_kernel(tc, table, w, b, ls, lb, offs, out):
+    nc = tc.nc
+    with (
+        tc.tile_pool(name="held", bufs=1) as held,
+        tc.tile_pool(name="work", bufs=2) as work,
+        tc.psum_pool(name="psum", bufs=1) as psum,
+    ):
+        offsets = held.tile([P, N // 16], U16, name="offsets")
+        nc.sync.dma_start(offsets[:], offs)
+        table_sb = held.tile([P, POINTS], BF16, name="table_sb")
+        nc.scalar.dma_start(table_sb[:], table)
+        w_sb = held.tile([P, P], BF16, name="w_sb")
+        nc.sync.dma_start(w_sb[:], w)
+        b_sb = held.tile([P, 1], F32, name="b_sb")
+        nc.sync.dma_start(b_sb[:], b)
+        b_all = held.tile([P, P], F32, name="b_all")
+        nc.scalar.dma_start(b_all[:], b.rearrange("m o -> (m o)").partition_broadcast(P))
+        ls_sb = held.tile([P, 1], F32, name="ls_sb")
+        nc.scalar.dma_start(ls_sb[:], ls)
+        lb_sb = held.tile([P, 1], F32, name="lb_sb")
+        nc.scalar.dma_start(lb_sb[:], lb)
+
+        mean_w = held.tile([P, P], BF16, name="mean_w")
+        nc.vector.memset(mean_w[:], 1.0 / P)
+        eps_sb = held.tile([P, 1], F32, name="eps_sb")
+        nc.vector.memset(eps_sb[:], EPS)
+
+        w_sum = held.tile([P, 1], F32, name="w_sum")
+        nc.vector.reduce_sum(w_sum[:], w_sb[:], axis=AX.X)
+        neg_mean_w = held.tile([P, P], BF16, name="neg_mean_w")
+        nc.vector.tensor_scalar_mul(neg_mean_w[:], w_sum[:, 0:1].to_broadcast([P, P]), -1.0 / P)
+
+        b_sum = held.tile([P, 1], F32, name="b_sum")
+        nc.vector.reduce_sum(b_sum[:], b_all[:], axis=AX.X)
+        bc = held.tile([P, 1], F32, name="bc")
+        nc.vector.scalar_tensor_tensor(bc[:], b_sum[:], -1.0 / P, b_sb[:], ALU.mult, ALU.add)
+
+        zc_ps = [psum.tile([P, CHUNK], F32, name=f"zc_ps{c}") for c in range(CHUNKS)]
+        for c in range(CHUNKS):
+            for h in range(CHUNK // PIECE):
+                first = (c * CHUNK + h * PIECE) // 16
+                looked_up = table_sb[:].indirect(offsets[:, first : first + PIECE // 16])
+                product = zc_ps[c][:, h * PIECE : (h + 1) * PIECE]
+                nc.tensor.matmul(product, w_sb[:], looked_up, start=True, stop=False)
+                nc.tensor.matmul(product, neg_mean_w[:], looked_up, start=False, stop=True)
+
+        sq = [held.tile([P, CHUNK], BF16, name=f"sq{c}") for c in range(CHUNKS)]
+        for c in range(CHUNKS):
+            nc.scalar.activation(sq[c][:], zc_ps[c][:], ACT.Square, bias=bc[:, 0:1])
+
+        for c in range(CHUNKS):
+            var_ps = psum.tile([P, CHUNK], F32, name=f"var_ps{c}")
+            nc.tensor.matmul(var_ps[:], mean_w[:], sq[c][:], start=True, stop=True)
+            rstd = work.tile([P, CHUNK], F32, name="rstd")
+            nc.scalar.activation(rstd[:], var_ps[:], ACT.Abs_reciprocal_sqrt, bias=eps_sb[:, 0:1])
+            zn = work.tile([P, CHUNK], F32, name="zn")
+            nc.vector.scalar_tensor_tensor(zn[:], zc_ps[c][:], bc[:, 0:1], rstd[:], ALU.add, ALU.mult)
+            y = work.tile([P, CHUNK], F32, name="y")
+            nc.scalar.activation(y[:], zn[:], ACT.Identity, bias=lb_sb[:, 0:1], scale=ls_sb[:, 0:1])
+            res = work.tile([P, CHUNK], F32, name="res")
+            nc.vector.scalar_tensor_tensor(res[:], y[:], SLOPE, y[:], ALU.mult, ALU.max)
+            nc.sync.dma_start(out[:, c * CHUNK : (c + 1) * CHUNK], res[:])

@@ -14,6 +14,8 @@ CHUNKS = N // CHUNK
 EPS = 1e-5
 SLOPE = 0.2
 
+WARM_MATMULS = 4
+
 FLOPS = 2 * P * P * N
 
 
@@ -23,6 +25,7 @@ def tile_lfa_kernel(tc, table, w, b, ls, lb, offs, out):
         tc.tile_pool(name="held", bufs=1) as held,
         tc.tile_pool(name="work", bufs=2) as work,
         tc.psum_pool(name="psum", bufs=1) as psum,
+        tc.psum_pool(name="psum_var", bufs=2) as psum_var,
     ):
         offsets = held.tile([P, N // 16], U16, name="offsets")
         nc.sync.dma_start(offsets[:], offs)
@@ -43,6 +46,12 @@ def tile_lfa_kernel(tc, table, w, b, ls, lb, offs, out):
         nc.vector.memset(mean_w[:], 1.0 / P)
         eps_sb = held.tile([P, 1], F32, name="eps_sb")
         nc.vector.memset(eps_sb[:], EPS)
+
+        zeros = held.tile([P, CHUNK], BF16, name="zeros")
+        nc.vector.memset(zeros[:], 0.0)
+        warm_ps = psum.tile([P, CHUNK], F32, name="warm_ps")
+        for i in range(WARM_MATMULS):
+            nc.tensor.matmul(warm_ps[:], mean_w[:], zeros[:], start=True, stop=True)
 
         w_sum = held.tile([P, 1], F32, name="w_sum")
         nc.vector.reduce_sum(w_sum[:], w_sb[:], axis=AX.X)
@@ -68,7 +77,7 @@ def tile_lfa_kernel(tc, table, w, b, ls, lb, offs, out):
             nc.scalar.activation(sq[c][:], zc_ps[c][:], ACT.Square, bias=bc[:, 0:1])
 
         for c in range(CHUNKS):
-            var_ps = psum.tile([P, CHUNK], F32, name=f"var_ps{c}")
+            var_ps = psum_var.tile([P, CHUNK], F32, name="var_ps")
             nc.tensor.matmul(var_ps[:], mean_w[:], sq[c][:], start=True, stop=True)
             rstd = work.tile([P, CHUNK], F32, name="rstd")
             nc.scalar.activation(rstd[:], var_ps[:], ACT.Abs_reciprocal_sqrt, bias=eps_sb[:, 0:1])

@@ -14,8 +14,6 @@ CHUNKS = N // CHUNK
 EPS = 1e-5
 SLOPE = 0.2
 
-WARM_MATMULS = 4
-
 FLOPS = 2 * P * P * N
 
 
@@ -23,9 +21,8 @@ def tile_lfa_kernel(tc, table, w, b, ls, lb, offs, out):
     nc = tc.nc
     with (
         tc.tile_pool(name="held", bufs=1) as held,
-        tc.tile_pool(name="work", bufs=2) as work,
+        tc.tile_pool(name="work", bufs=CHUNKS) as work,
         tc.psum_pool(name="psum", bufs=1) as psum,
-        tc.psum_pool(name="psum_var", bufs=2) as psum_var,
     ):
         offsets = held.tile([P, N // 16], U16, name="offsets")
         nc.sync.dma_start(offsets[:], offs)
@@ -46,12 +43,6 @@ def tile_lfa_kernel(tc, table, w, b, ls, lb, offs, out):
         nc.vector.memset(mean_w[:], 1.0 / P)
         eps_sb = held.tile([P, 1], F32, name="eps_sb")
         nc.vector.memset(eps_sb[:], EPS)
-
-        zeros = held.tile([P, CHUNK], BF16, name="zeros")
-        nc.vector.memset(zeros[:], 0.0)
-        warm_ps = psum.tile([P, CHUNK], F32, name="warm_ps")
-        for i in range(WARM_MATMULS):
-            nc.tensor.matmul(warm_ps[:], mean_w[:], zeros[:], start=True, stop=True)
 
         w_sum = held.tile([P, 1], F32, name="w_sum")
         nc.vector.reduce_sum(w_sum[:], w_sb[:], axis=AX.X)
@@ -76,15 +67,23 @@ def tile_lfa_kernel(tc, table, w, b, ls, lb, offs, out):
         for c in range(CHUNKS):
             nc.scalar.activation(sq[c][:], zc_ps[c][:], ACT.Square, bias=bc[:, 0:1])
 
+        rstd = [work.tile([P, CHUNK], F32, name="rstd") for c in range(CHUNKS)]
         for c in range(CHUNKS):
-            var_ps = psum_var.tile([P, CHUNK], F32, name="var_ps")
+            var_ps = psum.tile([P, CHUNK], F32, name=f"var_ps{c}")
             nc.tensor.matmul(var_ps[:], mean_w[:], sq[c][:], start=True, stop=True)
-            rstd = work.tile([P, CHUNK], F32, name="rstd")
-            nc.scalar.activation(rstd[:], var_ps[:], ACT.Abs_reciprocal_sqrt, bias=eps_sb[:, 0:1])
-            zn = work.tile([P, CHUNK], F32, name="zn")
-            nc.vector.scalar_tensor_tensor(zn[:], zc_ps[c][:], bc[:, 0:1], rstd[:], ALU.add, ALU.mult)
-            y = work.tile([P, CHUNK], F32, name="y")
-            nc.scalar.activation(y[:], zn[:], ACT.Identity, bias=lb_sb[:, 0:1], scale=ls_sb[:, 0:1])
-            res = work.tile([P, CHUNK], F32, name="res")
-            nc.vector.scalar_tensor_tensor(res[:], y[:], SLOPE, y[:], ALU.mult, ALU.max)
-            nc.sync.dma_start(out[:, c * CHUNK : (c + 1) * CHUNK], res[:])
+            nc.scalar.activation(rstd[c][:], var_ps[:], ACT.Abs_reciprocal_sqrt, bias=eps_sb[:, 0:1])
+
+        zn = [work.tile([P, CHUNK], F32, name="zn") for c in range(CHUNKS)]
+        y = [work.tile([P, CHUNK], F32, name="y") for c in range(CHUNKS)]
+        res = [work.tile([P, CHUNK], F32, name="res") for c in range(CHUNKS)]
+        for step in range(CHUNKS + 2):
+            if step < CHUNKS:
+                c = step
+                nc.vector.scalar_tensor_tensor(zn[c][:], zc_ps[c][:], bc[:, 0:1], rstd[c][:], ALU.add, ALU.mult)
+            if 1 <= step <= CHUNKS:
+                c = step - 1
+                nc.vector.tensor_scalar(y[c][:], zn[c][:], ls_sb[:, 0:1], lb_sb[:, 0:1], ALU.mult, ALU.add)
+            if 2 <= step:
+                c = step - 2
+                nc.vector.scalar_tensor_tensor(res[c][:], y[c][:], SLOPE, y[c][:], ALU.mult, ALU.max)
+                nc.sync.dma_start(out[:, c * CHUNK : (c + 1) * CHUNK], res[c][:])

@@ -67,23 +67,15 @@ def tile_lfa_kernel(tc, table, w, b, ls, lb, offs, out):
         for c in range(CHUNKS):
             nc.scalar.activation(sq[c][:], zc_ps[c][:], ACT.Square, bias=bc[:, 0:1])
 
-        rstd = [work.tile([P, CHUNK], F32, name="rstd") for c in range(CHUNKS)]
         for c in range(CHUNKS):
             var_ps = psum.tile([P, CHUNK], F32, name=f"var_ps{c}")
             nc.tensor.matmul(var_ps[:], mean_w[:], sq[c][:], start=True, stop=True)
-            nc.scalar.activation(rstd[c][:], var_ps[:], ACT.Abs_reciprocal_sqrt, bias=eps_sb[:, 0:1])
-
-        zn = [work.tile([P, CHUNK], F32, name="zn") for c in range(CHUNKS)]
-        y = [work.tile([P, CHUNK], F32, name="y") for c in range(CHUNKS)]
-        res = [work.tile([P, CHUNK], F32, name="res") for c in range(CHUNKS)]
-        for step in range(CHUNKS + 2):
-            if step < CHUNKS:
-                c = step
-                nc.vector.scalar_tensor_tensor(zn[c][:], zc_ps[c][:], bc[:, 0:1], rstd[c][:], ALU.add, ALU.mult)
-            if 1 <= step <= CHUNKS:
-                c = step - 1
-                nc.vector.tensor_scalar(y[c][:], zn[c][:], ls_sb[:, 0:1], lb_sb[:, 0:1], ALU.mult, ALU.add)
-            if 2 <= step:
-                c = step - 2
-                nc.vector.scalar_tensor_tensor(res[c][:], y[c][:], SLOPE, y[c][:], ALU.mult, ALU.max)
-                nc.sync.dma_start(out[:, c * CHUNK : (c + 1) * CHUNK], res[c][:])
+            rstd = work.tile([P, CHUNK], F32, name="rstd")
+            nc.scalar.activation(rstd[:], var_ps[:], ACT.Abs_reciprocal_sqrt, bias=eps_sb[:, 0:1])
+            zn = work.tile([P, CHUNK], F32, name="zn")
+            nc.vector.scalar_tensor_tensor(zn[:], zc_ps[c][:], bc[:, 0:1], rstd[:], ALU.add, ALU.mult)
+            y = work.tile([P, CHUNK], F32, name="y")
+            nc.scalar.activation(y[:], zn[:], ACT.Identity, bias=lb_sb[:, 0:1], scale=ls_sb[:, 0:1])
+            res = work.tile([P, CHUNK], F32, name="res")
+            nc.vector.scalar_tensor_tensor(res[:], y[:], SLOPE, y[:], ALU.mult, ALU.max)
+            nc.sync.dma_start(out[:, c * CHUNK : (c + 1) * CHUNK], res[:])

@@ -44,6 +44,9 @@ def tile_lfa_kernel(tc, table, w, b, ls, lb, offs, out):
         eps_sb = held.tile([P, 1], F32, name="eps_sb")
         nc.vector.memset(eps_sb[:], EPS)
 
+        warm = held.tile([P, 1], F32, name="warm")
+        nc.scalar.activation(warm[:], eps_sb[:], ACT.Abs_reciprocal_sqrt)
+
         w_sum = held.tile([P, 1], F32, name="w_sum")
         nc.vector.reduce_sum(w_sum[:], w_sb[:], axis=AX.X)
         neg_mean_w = held.tile([P, P], BF16, name="neg_mean_w")

@@ -11,6 +11,7 @@ N = 2048
 PIECE = 256
 CHUNK = 512
 CHUNKS = N // CHUNK
+STEP = 256
 EPS = 1e-5
 SLOPE = 0.2
 
@@ -21,7 +22,7 @@ def tile_lfa_kernel(tc, table, w, b, ls, lb, offs, out):
     nc = tc.nc
     with (
         tc.tile_pool(name="held", bufs=1) as held,
-        tc.tile_pool(name="work", bufs=CHUNKS) as work,
+        tc.tile_pool(name="work", bufs=N // STEP) as work,
         tc.psum_pool(name="psum", bufs=1) as psum,
     ):
         offsets = held.tile([P, N // 16], U16, name="offsets")
@@ -73,12 +74,15 @@ def tile_lfa_kernel(tc, table, w, b, ls, lb, offs, out):
         for c in range(CHUNKS):
             var_ps = psum.tile([P, CHUNK], F32, name=f"var_ps{c}")
             nc.tensor.matmul(var_ps[:], mean_w[:], sq[c][:], start=True, stop=True)
-            rstd = work.tile([P, CHUNK], F32, name="rstd")
-            nc.scalar.activation(rstd[:], var_ps[:], ACT.Abs_reciprocal_sqrt, bias=eps_sb[:, 0:1])
-            zn = work.tile([P, CHUNK], F32, name="zn")
-            nc.vector.scalar_tensor_tensor(zn[:], zc_ps[c][:], bc[:, 0:1], rstd[:], ALU.add, ALU.mult)
-            y = work.tile([P, CHUNK], F32, name="y")
-            nc.scalar.activation(y[:], zn[:], ACT.Identity, bias=lb_sb[:, 0:1], scale=ls_sb[:, 0:1])
-            res = work.tile([P, CHUNK], F32, name="res")
-            nc.vector.scalar_tensor_tensor(res[:], y[:], SLOPE, y[:], ALU.mult, ALU.max)
-            nc.sync.dma_start(out[:, c * CHUNK : (c + 1) * CHUNK], res[:])
+            for s in range(CHUNK // STEP):
+                cols = slice(s * STEP, (s + 1) * STEP)
+                rstd = work.tile([P, STEP], F32, name="rstd")
+                nc.scalar.activation(rstd[:], var_ps[:, cols], ACT.Abs_reciprocal_sqrt, bias=eps_sb[:, 0:1])
+                zn = work.tile([P, STEP], F32, name="zn")
+                nc.vector.scalar_tensor_tensor(zn[:], zc_ps[c][:, cols], bc[:, 0:1], rstd[:], ALU.add, ALU.mult)
+                y = work.tile([P, STEP], F32, name="y")
+                nc.scalar.activation(y[:], zn[:], ACT.Identity, bias=lb_sb[:, 0:1], scale=ls_sb[:, 0:1])
+                res = work.tile([P, STEP], F32, name="res")
+                nc.vector.scalar_tensor_tensor(res[:], y[:], SLOPE, y[:], ALU.mult, ALU.max)
+                first = c * CHUNK + s * STEP
+                nc.sync.dma_start(out[:, first : first + STEP], res[:])

@@ -9,9 +9,10 @@ P = 128
 POINTS = 256
 N = 2048
 PIECE = 256
-CHUNK = 512
-CHUNKS = N // CHUNK
+WIDTHS = (512, 512, 512, 256, 256)
+STARTS = tuple(sum(WIDTHS[:c]) for c in range(len(WIDTHS)))
 STEP = 256
+VAR_BANKS = 8 - len(WIDTHS)
 EPS = 1e-5
 SLOPE = 0.2
 
@@ -24,6 +25,7 @@ def tile_lfa_kernel(tc, table, w, b, ls, lb, offs, out):
         tc.tile_pool(name="held", bufs=1) as held,
         tc.tile_pool(name="work", bufs=N // STEP) as work,
         tc.psum_pool(name="psum", bufs=1) as psum,
+        tc.psum_pool(name="var_pool", bufs=VAR_BANKS) as var_pool,
     ):
         offsets = held.tile([P, N // 16], U16, name="offsets")
         nc.sync.dma_start(offsets[:], offs)
@@ -58,23 +60,23 @@ def tile_lfa_kernel(tc, table, w, b, ls, lb, offs, out):
         bc = held.tile([P, 1], F32, name="bc")
         nc.vector.scalar_tensor_tensor(bc[:], b_sum[:], -1.0 / P, b_sb[:], ALU.mult, ALU.add)
 
-        zc_ps = [psum.tile([P, CHUNK], F32, name=f"zc_ps{c}") for c in range(CHUNKS)]
-        for c in range(CHUNKS):
-            for h in range(CHUNK // PIECE):
-                first = (c * CHUNK + h * PIECE) // 16
+        zc_ps = [psum.tile([P, width], F32, name=f"zc_ps{c}") for c, width in enumerate(WIDTHS)]
+        for c, width in enumerate(WIDTHS):
+            for h in range(width // PIECE):
+                first = (STARTS[c] + h * PIECE) // 16
                 looked_up = table_sb[:].indirect(offsets[:, first : first + PIECE // 16])
                 product = zc_ps[c][:, h * PIECE : (h + 1) * PIECE]
                 nc.tensor.matmul(product, w_sb[:], looked_up, start=True, stop=False)
                 nc.tensor.matmul(product, neg_mean_w[:], looked_up, start=False, stop=True)
 
-        sq = [held.tile([P, CHUNK], BF16, name=f"sq{c}") for c in range(CHUNKS)]
-        for c in range(CHUNKS):
+        sq = [held.tile([P, width], BF16, name=f"sq{c}") for c, width in enumerate(WIDTHS)]
+        for c in range(len(WIDTHS)):
             nc.scalar.activation(sq[c][:], zc_ps[c][:], ACT.Square, bias=bc[:, 0:1])
 
-        for c in range(CHUNKS):
-            var_ps = psum.tile([P, CHUNK], F32, name=f"var_ps{c}")
+        for c, width in enumerate(WIDTHS):
+            var_ps = var_pool.tile([P, width], F32, name="var_ps")
             nc.tensor.matmul(var_ps[:], mean_w[:], sq[c][:], start=True, stop=True)
-            for s in range(CHUNK // STEP):
+            for s in range(width // STEP):
                 cols = slice(s * STEP, (s + 1) * STEP)
                 rstd = work.tile([P, STEP], F32, name="rstd")
                 nc.scalar.activation(rstd[:], var_ps[:, cols], ACT.Abs_reciprocal_sqrt, bias=eps_sb[:, 0:1])
@@ -84,5 +86,5 @@ def tile_lfa_kernel(tc, table, w, b, ls, lb, offs, out):
                 nc.scalar.activation(y[:], zn[:], ACT.Identity, bias=lb_sb[:, 0:1], scale=ls_sb[:, 0:1])
                 res = work.tile([P, STEP], F32, name="res")
                 nc.vector.scalar_tensor_tensor(res[:], y[:], SLOPE, y[:], ALU.mult, ALU.max)
-                first = c * CHUNK + s * STEP
+                first = STARTS[c] + s * STEP
                 nc.sync.dma_start(out[:, first : first + STEP], res[:])

@@ -33,14 +33,14 @@ def tile_lfa_kernel(tc, table, w, b, ls, lb, offs, out):
         nc.scalar.dma_start(table_sb[:], table)
         w_sb = held.tile([P, P], BF16, name="w_sb")
         nc.sync.dma_start(w_sb[:], w)
+        b_all = held.tile([P, P], F32, name="b_all")
+        nc.sync.dma_start(b_all[:], b.rearrange("m o -> (m o)").partition_broadcast(P))
         b_sb = held.tile([P, 1], F32, name="b_sb")
         nc.sync.dma_start(b_sb[:], b)
-        b_all = held.tile([P, P], F32, name="b_all")
-        nc.scalar.dma_start(b_all[:], b.rearrange("m o -> (m o)").partition_broadcast(P))
         ls_sb = held.tile([P, 1], F32, name="ls_sb")
-        nc.scalar.dma_start(ls_sb[:], ls)
+        nc.sync.dma_start(ls_sb[:], ls)
         lb_sb = held.tile([P, 1], F32, name="lb_sb")
-        nc.scalar.dma_start(lb_sb[:], lb)
+        nc.sync.dma_start(lb_sb[:], lb)
 
         mean_w = held.tile([P, P], BF16, name="mean_w")
         nc.vector.memset(mean_w[:], 1.0 / P)

@@ -30,7 +30,7 @@ def tile_lfa_kernel(tc, table, w, b, ls, lb, offs, out):
         offsets = held.tile([P, N // 16], U16, name="offsets")
         nc.sync.dma_start(offsets[:], offs)
         table_sb = held.tile([P, POINTS], BF16, name="table_sb")
-        nc.scalar.dma_start(table_sb[:], table)
+        nc.sync.dma_start(table_sb[:], table)
         w_sb = held.tile([P, P], BF16, name="w_sb")
         nc.sync.dma_start(w_sb[:], w)
         b_all = held.tile([P, P], F32, name="b_all")

@@ -12,6 +12,7 @@ PIECE = 256
 WIDTHS = (512, 512, 512, 256, 256)
 STARTS = tuple(sum(WIDTHS[:c]) for c in range(len(WIDTHS)))
 STEP = 256
+VECTOR_SQUARES = 2
 VAR_BANKS = 8 - len(WIDTHS)
 EPS = 1e-5
 SLOPE = 0.2
@@ -70,8 +71,13 @@ def tile_lfa_kernel(tc, table, w, b, ls, lb, offs, out):
                 nc.tensor.matmul(product, neg_mean_w[:], looked_up, start=False, stop=True)
 
         sq = [held.tile([P, width], BF16, name=f"sq{c}") for c, width in enumerate(WIDTHS)]
-        for c in range(len(WIDTHS)):
-            nc.scalar.activation(sq[c][:], zc_ps[c][:], ACT.Square, bias=bc[:, 0:1])
+        for c, width in enumerate(WIDTHS):
+            if c == VECTOR_SQUARES:
+                zc = held.tile([P, width], F32, name="zc")
+                nc.vector.tensor_scalar_add(zc[:], zc_ps[c][:], bc[:, 0:1])
+                nc.vector.tensor_tensor(sq[c][:], zc[:], zc[:], ALU.mult)
+            else:
+                nc.scalar.activation(sq[c][:], zc_ps[c][:], ACT.Square, bias=bc[:, 0:1])
 
         for c, width in enumerate(WIDTHS):
             var_ps = var_pool.tile([P, width], F32, name="var_ps")

import concourse.mybir as mybir

F32, BF16, U16 = mybir.dt.float32, mybir.dt.bfloat16, mybir.dt.uint16
ACT = mybir.ActivationFunctionType
ALU = mybir.AluOpType
AX = mybir.AxisListType

P = 128
POINTS = 256
N = 2048
PIECE = 256
WIDTHS = (512, 512, 512, 256, 256)
STARTS = tuple(sum(WIDTHS[:c]) for c in range(len(WIDTHS)))
STEP = 256
VECTOR_SQUARES = 2
VAR_BANKS = 8 - len(WIDTHS)
EPS = 1e-5
SLOPE = 0.2

FLOPS = 2 * P * P * N


def tile_lfa_kernel(tc, table, w, b, ls, lb, offs, out):
    nc = tc.nc
    with (
        tc.tile_pool(name="held", bufs=1) as held,
        tc.tile_pool(name="work", bufs=N // STEP) as work,
        tc.psum_pool(name="psum", bufs=1) as psum,
        tc.psum_pool(name="var_pool", bufs=VAR_BANKS) as var_pool,
    ):
        offsets = held.tile([P, N // 16], U16, name="offsets")
        nc.sync.dma_start(offsets[:], offs)
        table_sb = held.tile([P, POINTS], BF16, name="table_sb")
        nc.sync.dma_start(table_sb[:], table)
        w_sb = held.tile([P, P], BF16, name="w_sb")
        nc.sync.dma_start(w_sb[:], w)
        b_all = held.tile([P, P], F32, name="b_all")
        nc.sync.dma_start(b_all[:], b.rearrange("m o -> (m o)").partition_broadcast(P))
        b_sb = held.tile([P, 1], F32, name="b_sb")
        nc.sync.dma_start(b_sb[:], b)
        ls_sb = held.tile([P, 1], F32, name="ls_sb")
        nc.sync.dma_start(ls_sb[:], ls)
        lb_sb = held.tile([P, 1], F32, name="lb_sb")
        nc.sync.dma_start(lb_sb[:], lb)

        mean_w = held.tile([P, P], BF16, name="mean_w")
        nc.vector.memset(mean_w[:], 1.0 / P)
        eps_sb = held.tile([P, 1], F32, name="eps_sb")
        nc.vector.memset(eps_sb[:], EPS)

        warm = held.tile([P, 1], F32, name="warm")
        nc.scalar.activation(warm[:], eps_sb[:], ACT.Abs_reciprocal_sqrt)

        w_sum = held.tile([P, 1], F32, name="w_sum")
        nc.vector.reduce_sum(w_sum[:], w_sb[:], axis=AX.X)
        neg_mean_w = held.tile([P, P], BF16, name="neg_mean_w")
        nc.vector.tensor_scalar_mul(neg_mean_w[:], w_sum[:, 0:1].to_broadcast([P, P]), -1.0 / P)

        b_sum = held.tile([P, 1], F32, name="b_sum")
        nc.vector.reduce_sum(b_sum[:], b_all[:], axis=AX.X)
        bc = held.tile([P, 1], F32, name="bc")
        nc.vector.scalar_tensor_tensor(bc[:], b_sum[:], -1.0 / P, b_sb[:], ALU.mult, ALU.add)

        zc_ps = [psum.tile([P, width], F32, name=f"zc_ps{c}") for c, width in enumerate(WIDTHS)]
        for c, width in enumerate(WIDTHS):
            for h in range(width // PIECE):
                first = (STARTS[c] + h * PIECE) // 16
                looked_up = table_sb[:].indirect(offsets[:, first : first + PIECE // 16])
                product = zc_ps[c][:, h * PIECE : (h + 1) * PIECE]
                nc.tensor.matmul(product, w_sb[:], looked_up, start=True, stop=False)
                nc.tensor.matmul(product, neg_mean_w[:], looked_up, start=False, stop=True)

        sq = [held.tile([P, width], BF16, name=f"sq{c}") for c, width in enumerate(WIDTHS)]
        for c, width in enumerate(WIDTHS):
            if c == VECTOR_SQUARES:
                zc = held.tile([P, width], F32, name="zc")
                nc.vector.tensor_scalar_add(zc[:], zc_ps[c][:], bc[:, 0:1])
                nc.vector.tensor_tensor(sq[c][:], zc[:], zc[:], ALU.mult)
            else:
                nc.scalar.activation(sq[c][:], zc_ps[c][:], ACT.Square, bias=bc[:, 0:1])

        for c, width in enumerate(WIDTHS):
            var_ps = var_pool.tile([P, width], F32, name="var_ps")
            nc.tensor.matmul(var_ps[:], mean_w[:], sq[c][:], start=True, stop=True)
            for s in range(width // STEP):
                cols = slice(s * STEP, (s + 1) * STEP)
                rstd = work.tile([P, STEP], F32, name="rstd")
                nc.scalar.activation(rstd[:], var_ps[:, cols], ACT.Abs_reciprocal_sqrt, bias=eps_sb[:, 0:1])
                zn = work.tile([P, STEP], F32, name="zn")
                nc.vector.scalar_tensor_tensor(zn[:], zc_ps[c][:, cols], bc[:, 0:1], rstd[:], ALU.add, ALU.mult)
                y = work.tile([P, STEP], F32, name="y")
                nc.scalar.activation(y[:], zn[:], ACT.Identity, bias=lb_sb[:, 0:1], scale=ls_sb[:, 0:1])
                res = work.tile([P, STEP], F32, name="res")
                nc.vector.scalar_tensor_tensor(res[:], y[:], SLOPE, y[:], ALU.mult, ALU.max)
                first = STARTS[c] + s * STEP
                nc.sync.dma_start(out[:, first : first + STEP], res[:])
